import numpy as np
import ml_dtypes


def mxq(x, axis, fmt="e4m3"):
    dtype, down = {"e4m3": (ml_dtypes.float8_e4m3fn, 7), "e5m2": (ml_dtypes.float8_e5m2, 14)}[fmt]
    v = np.moveaxis(np.asarray(x, np.float32).astype(ml_dtypes.bfloat16).astype(np.float64), axis, -1)
    blocks = v.reshape(v.shape[:-1] + (-1, 32))
    amax = np.abs(blocks).max(-1, keepdims=True)
    byte = np.maximum(np.where(amax > 0, np.frexp(amax)[1] - 1 + 127, 0) - down, 1)
    scale = np.exp2(byte - 127.0)
    codes = (blocks / scale).astype(np.float32).astype(dtype).astype(np.float64)
    return np.moveaxis((codes * scale).reshape(v.shape), -1, axis)


WIDE = False


def mx_kscale(k):
    if not WIDE:
        return np.ones(k)
    levels = np.array([10, -10, 5, -5, 0])
    if k % 512:
        return np.exp2(np.random.permutation(np.resize(levels, k // 32))).repeat(32)
    a = np.empty((k // 512, 16))
    for p in range(k // 512):
        a[p, :8] = np.random.permutation(np.resize(levels, 8))
        for g in range(8):
            far = levels[np.abs(levels - a[p, g]) >= 10]
            a[p, g + 8] = far[np.random.randint(len(far))]
    return np.exp2(a.ravel()).repeat(32)


BF16 = ml_dtypes.bfloat16


def bf(x):
    return np.asarray(x, np.float32).astype(BF16)


def f64(x):
    return np.asarray(x).astype(np.float64)


B, I, H = 1024, 1024, 1024
G = 2 * H
EPS = 1e-5


def ln(v):
    mu = v.mean(-1, keepdims=True)
    var = np.square(v - mu).mean(-1, keepdims=True)
    return (v - mu) / np.sqrt(var + EPS)


def sigmoid(v):
    return 1.0 / (1.0 + np.exp(-v))


def setup_inputs():
    s, t = mx_kscale(I), mx_kscale(H)
    return {"x": bf(np.random.standard_normal((B, I)) * s),
            "h": bf(np.random.standard_normal((B, H)) * t),
            "W_irz": bf(np.random.standard_normal((G, I)) / np.sqrt(I) / s),
            "b_irz": bf(np.random.standard_normal(G) * 0.5),
            "W_hrz": bf(np.random.standard_normal((G, H)) / np.sqrt(H) / t),
            "b_hrz": bf(np.random.standard_normal(G) * 0.5)}


def core(x, h, W_irz, b_irz, W_hrz, b_hrz):
    i_rz = ln((mxq(f64(x), 1, "e4m3") @ mxq(f64(W_irz), 1, "e4m3").T) + f64(b_irz))
    h_rz = ln((mxq(f64(h), 1, "e4m3") @ mxq(f64(W_hrz), 1, "e4m3").T) + f64(b_hrz))
    return sigmoid(i_rz + h_rz)


def e4m3fn_bytes(y):
    return np.clip(np.asarray(y, np.float64), -448.0, 448.0).astype(np.float32).astype(ml_dtypes.float8_e4m3fn).view(np.uint8)


def reference(x, h, W_irz, b_irz, W_hrz, b_hrz):
    out = core(x, h, W_irz, b_irz, W_hrz, b_hrz)
    s = np.max(np.abs(out)) / 448.0
    return out, e4m3fn_bytes(out / s)

@@ -1,0 +1,260 @@
+from contextlib import ExitStack
+
+import concourse.mybir as mybir
+from concourse.masks import make_identity
+
+F32 = mybir.dt.float32
+BF16 = mybir.dt.bfloat16
+U32 = mybir.dt.uint32
+U8 = mybir.dt.uint8
+FP8X4 = mybir.dt.float8_e4m3fn_x4
+FP8 = mybir.dt.float8_e4m3fn
+AF = mybir.ActivationFunctionType
+OP = mybir.AluOpType
+AX = mybir.AxisListType
+
+P = 128
+ROWS = 1024
+K = 1024
+N = 2048
+EPS = 1e-5
+FLOPS = 2 * 2 * ROWS * K * N
+M_TILES = ROWS // P
+N_BANKS = N // 512
+CV = 1344
+
+
+def tile_layernormgrucell_pa_kernel(tc, x, h, W_irz, b_irz, W_hrz, b_hrz, out_0, out_1):
+    nc = tc.nc
+    with ExitStack() as ctx:
+        keep = ctx.enter_context(tc.tile_pool(name="keep", bufs=1))
+        stat = ctx.enter_context(tc.tile_pool(name="stat", bufs=4))
+        psum = ctx.enter_context(tc.psum_pool(name="psum", bufs=8))
+
+        ident = keep.tile([P, P], F32, name="ident")
+        make_identity(nc, ident[:])
+        mhalf = keep.tile([P, 2], F32, name="mhalf")
+        nc.gpsimd.memset(mhalf[:], -0.5)
+        warm_in = keep.tile([P, 1], F32, name="warm_in")
+        nc.gpsimd.memset(warm_in[:], 0.0)
+        warm_out = keep.tile([P, 1], F32, name="warm_out")
+        nc.scalar.activation(out=warm_out[:], in_=warm_in[:], func=AF.Sigmoid)
+        pmax = keep.tile([P, M_TILES], F32, name="pmax")
+        o = [keep.tile([P, N], F32, name="o%d" % m) for m in range(M_TILES)]
+
+        with ExitStack() as work:
+            codes = work.enter_context(tc.tile_pool(name="codes", bufs=1))
+            raw = work.enter_context(tc.tile_pool(name="raw", bufs=8))
+            gqp = work.enter_context(tc.tile_pool(name="gqp", bufs=4))
+            zpool = work.enter_context(tc.tile_pool(name="zpool", bufs=3))
+            junkp = work.enter_context(tc.tile_pool(name="junkp", bufs=2))
+
+            wc = [codes.tile([P, 2, N], U32, name="wc%d" % s, align_bytes=64) for s in range(2)]
+            ws = [codes.tile([P, 2, N], U8, name="ws%d" % s, align_bytes=64) for s in range(2)]
+            xc = [codes.tile([P, 2, ROWS], U32, name="xc%d" % s, align_bytes=64) for s in range(2)]
+            xs = [codes.tile([P, 2, ROWS], U8, name="xs%d" % s, align_bytes=64) for s in range(2)]
+            bias = [codes.tile([P, N], BF16, name="bias%d" % s) for s in range(2)]
+
+            groups = []
+            for gi in range(4):
+                groups.append((W_irz, wc[0], ws[0], gi))
+            for gi in range(2):
+                groups.append((x, xc[0], xs[0], gi))
+            for gi in range(4):
+                groups.append((W_hrz, wc[1], ws[1], gi))
+            for gi in range(2):
+                groups.append((h, xc[1], xs[1], gi))
+            n_groups = len(groups)
+            rawt = {}
+            banks = {}
+            gq = {}
+
+            def load(k):
+                src = groups[k][0]
+                gi = groups[k][3]
+                for j in range(2):
+                    r = raw.tile([P, 2, K], BF16, name="raw", tag="raw")
+                    r0 = (4 * gi + 2 * j) * P
+                    nc.sync.dma_start(out=r[:], in_=src[r0:r0 + 2 * P, :].rearrange("(t p) k -> p t k", p=P))
+                    rawt[(k, j)] = r
+
+            def transposes(k):
+                for j in range(2):
+                    words = rawt[(k, j)][:].bitcast(F32)
+                    for g in range(2):
+                        bank = psum.tile([P, 2, 2, P], F32, name="bank", tag="bank")
+                        for t in range(2):
+                            for u in range(2):
+                                nc.tensor.transpose(bank[:, t, u, :], words[:, t, 256 * g + u:256 * (g + 1):2], ident[:])
+                        banks[(k, j, g)] = bank
+
+            def evac(k, j, g, on_vector):
+                if (k, g) not in gq:
+                    gq[(k, g)] = gqp.tile([P, 2048], BF16, name="gq", tag="gq", align_bytes=64)
+                dst = gq[(k, g)][:, 1024 * j:1024 * (j + 1)].bitcast(F32).rearrange("p (t r u) -> p t r u", t=2, u=2)
+                src = banks[(k, j, g)][:].rearrange("p t u r -> p t r u")
+                if on_vector:
+                    nc.vector.tensor_copy(out=dst, in_=src)
+                else:
+                    nc.scalar.copy(out=dst, in_=src)
+
+            def quant(k, g):
+                cod = groups[k][1]
+                sca = groups[k][2]
+                c0 = 512 * groups[k][3]
+                nc.vector.quantize_mx(out=cod[:, g, c0:c0 + 512].bitcast(FP8X4), scales=sca[:, g, c0:c0 + 512], in_=gq[(k, g)][:])
+
+            def finish(k):
+                evac(k, 0, 0, False)
+                evac(k, 0, 1, False)
+                evac(k, 1, 0, False)
+                evac(k, 1, 1, True)
+                quant(k, 0)
+                quant(k, 1)
+
+            acc = {}
+            zh = {}
+            sums = {}
+            negmean = {}
+            ssq = {}
+            rr = {}
+            cc = {}
+            qq = {}
+
+            def mx(m, s):
+                tiles = [psum.tile([P, 512], F32, name="acc", tag="bank") for n in range(N_BANKS)]
+                for g in range(2):
+                    for n in range(N_BANKS):
+                        nc.tensor.matmul_mx(
+                            out=tiles[n][:],
+                            lhsT=xc[s][:, g, P * m:P * (m + 1)].bitcast(FP8X4),
+                            lhsT_scale=xs[s][:, g, P * m:P * (m + 1)],
+                            rhs=wc[s][:, g, 512 * n:512 * (n + 1)].bitcast(FP8X4),
+                            rhs_scale=ws[s][:, g, 512 * n:512 * (n + 1)],
+                            start=(g == 0),
+                            stop=(g == 1),
+                        )
+                acc[(m, s)] = tiles
+
+            def evac_z(m, s):
+                if s == 0:
+                    sums[m] = stat.tile([P, 8], F32, name="sums", tag="sums")
+                    negmean[m] = stat.tile([P, 2], F32, name="negmean", tag="negmean")
+                    ssq[m] = stat.tile([P, 2], F32, name="ssq", tag="ssq")
+                    z = o[m]
+                else:
+                    zh[m] = zpool.tile([P, N], F32, name="zh", tag="zh")
+                    z = zh[m]
+                for n in range(N_BANKS):
+                    nc.vector.scalar_tensor_tensor(
+                        out=z[:, 512 * n:512 * (n + 1)], in0=acc[(m, s)][n][:], scalar=1.0,
+                        in1=bias[s][:, 512 * n:512 * (n + 1)], op0=OP.mult, op1=OP.add,
+                        accum_out=sums[m][:, 4 * s + n:4 * s + n + 1])
+                scr = stat.tile([P, 4], F32, name="scr", tag="scr")
+                nc.vector.tensor_scalar(
+                    out=scr[:], in0=sums[m][:, 4 * s:4 * s + 4], scalar1=-1.0 / N, scalar2=None,
+                    op0=OP.mult, op1=OP.add, accum_out=negmean[m][:, s:s + 1])
+
+            def square(m, s):
+                z = o[m] if s == 0 else zh[m]
+                junk = junkp.tile([P, N], BF16, name="junk", tag="junk")
+                nc.scalar.activation(out=junk[:], in_=z[:], func=AF.Square, bias=negmean[m][:, s:s + 1], scale=1.0,
+                                     accum_out=ssq[m][:, s:s + 1])
+
+            def chain(m):
+                ve = stat.tile([P, 2], F32, name="ve", tag="ve")
+                nc.gpsimd.tensor_scalar(out=ve[:], in0=ssq[m][:], scalar1=1.0 / N, scalar2=EPS, op0=OP.mult, op1=OP.add)
+                r = stat.tile([P, 2], F32, name="r", tag="r")
+                nc.gpsimd.tensor_tensor(out=r[:], in0=ve[:], in1=mhalf[:], op=OP.pow)
+                pr = stat.tile([P, 2], F32, name="pr", tag="pr")
+                nc.gpsimd.tensor_tensor(out=pr[:], in0=negmean[m][:], in1=r[:], op=OP.mult)
+                c = stat.tile([P, 1], F32, name="c", tag="c")
+                nc.gpsimd.tensor_tensor(out=c[:], in0=pr[:, 0:1], in1=pr[:, 1:2], op=OP.add)
+                a = stat.tile([P, 1], F32, name="a", tag="a")
+                nc.gpsimd.tensor_tensor(out=a[:], in0=r[:, 0:1], in1=r[:, 1:2], op=OP.mult)
+                q = stat.tile([P, 1], F32, name="q", tag="q")
+                nc.gpsimd.tensor_tensor(out=q[:], in0=a[:], in1=ve[:, 1:2], op=OP.mult)
+                rr[m] = r
+                cc[m] = c
+                qq[m] = q
+
+            def comb(m):
+                nc.vector.scalar_tensor_tensor(out=o[m][:], in0=o[m][:], scalar=qq[m][:, 0:1], in1=zh[m][:],
+                                               op0=OP.mult, op1=OP.add)
+
+            def sig(m):
+                nc.scalar.activation(out=o[m][:], in_=o[m][:], func=AF.Sigmoid, scale=rr[m][:, 1:2], bias=cc[m][:, 0:1])
+                nc.sync.dma_start(out=out_0[P * m:P * (m + 1), :], in_=o[m][:])
+
+            def amax(m):
+                nc.vector.tensor_reduce(out=pmax[:, m:m + 1], in_=o[m][:], op=OP.max, axis=AX.X, apply_absolute_value=True)
+
+            for k in range(4):
+                load(k)
+            transposes(0)
+            transposes(1)
+            for k in range(n_groups):
+                finish(k)
+                if k + 4 < n_groups:
+                    load(k + 4)
+                if k + 4 == n_groups:
+                    nc.sync.dma_start(out=bias[0][:], in_=b_irz.partition_broadcast(P))
+                    nc.sync.dma_start(out=bias[1][:], in_=b_hrz.partition_broadcast(P))
+                if k + 2 < n_groups:
+                    transposes(k + 2)
+                if k + 2 == n_groups:
+                    mx(0, 0)
+            mx(0, 1)
+
+            for m in range(M_TILES):
+                evac_z(m, 0)
+                square(m, 0)
+                if m + 1 < M_TILES:
+                    mx(m + 1, 0)
+                if m >= 2:
+                    amax(m - 2)
+                evac_z(m, 1)
+                square(m, 1)
+                if m + 1 < M_TILES:
+                    mx(m + 1, 1)
+                chain(m)
+                if m >= 1:
+                    comb(m - 1)
+                    sig(m - 1)
+            amax(M_TILES - 2)
+            comb(M_TILES - 1)
+            sig(M_TILES - 1)
+            amax(M_TILES - 1)
+
+        part = stat.tile([P, 1], F32, name="part", tag="part")
+        nc.vector.tensor_reduce(out=part[:], in_=pmax[:], op=OP.max, axis=AX.X)
+        spread = psum.tile([P, 512], F32, name="spread", tag="bank")
+        nc.tensor.transpose(spread[:, 0:P], part[:, 0:1].to_broadcast([P, P]), ident[:])
+        top = stat.tile([P, 1], F32, name="top", tag="top")
+        nc.vector.tensor_reduce(out=top[:], in_=spread[:, 0:P], op=OP.max, axis=AX.X)
+        rec = stat.tile([P, 1], F32, name="rec", tag="rec")
+        nc.vector.reciprocal(out=rec[:], in_=top[:])
+        fac = stat.tile([P, 1], F32, name="fac", tag="fac")
+        nc.vector.tensor_scalar(out=fac[:], in0=rec[:], scalar1=448.0, scalar2=None, op0=OP.mult)
+
+        scp = ctx.enter_context(tc.tile_pool(name="scp", bufs=3))
+        o8p = ctx.enter_context(tc.tile_pool(name="o8p", bufs=4))
+        sc = {}
+        o8 = {}
+
+        def scale2(m):
+            sc[m] = scp.tile([P, N], F32, name="sc", tag="sc")
+            nc.vector.tensor_scalar(out=sc[m][:, 0:CV], in0=o[m][:, 0:CV], scalar1=fac[:, 0:1], scalar2=None, op0=OP.mult)
+            nc.scalar.activation(out=sc[m][:, CV:N], in_=o[m][:, CV:N], func=AF.Copy, scale=fac[:, 0:1])
+
+        def cast2(m):
+            o8[m] = o8p.tile([P, N], FP8, name="o8", tag="o8")
+            nc.vector.tensor_copy(out=o8[m][:, 0:CV], in_=sc[m][:, 0:CV], saturate=False)
+            nc.scalar.copy(out=o8[m][:, CV:N], in_=sc[m][:, CV:N], saturate=False)
+            nc.sync.dma_start(out=out_1[P * m:P * (m + 1), :], in_=o8[m][:].bitcast(U8))
+
+        scale2(0)
+        for m in range(M_TILES):
+            if m + 1 < M_TILES:
+                scale2(m + 1)
+            cast2(m)

@@ -7,6 +7,7 @@ F32 = mybir.dt.float32
 BF16 = mybir.dt.bfloat16
 U32 = mybir.dt.uint32
 U8 = mybir.dt.uint8
+I32 = mybir.dt.int32
 FP8X4 = mybir.dt.float8_e4m3fn_x4
 FP8 = mybir.dt.float8_e4m3fn
 AF = mybir.ActivationFunctionType
@@ -22,13 +23,15 @@ FLOPS = 2 * 2 * ROWS * K * N
 M_TILES = ROWS // P
 N_BANKS = N // 512
 CV = 1344
+FORMS = ("V", "V", "V", "V", "V", "V", "V", "V")
+ET_ON_VECTOR = (False, False, False, True)
 
 
 def tile_layernormgrucell_pa_kernel(tc, x, h, W_irz, b_irz, W_hrz, b_hrz, out_0, out_1):
     nc = tc.nc
     with ExitStack() as ctx:
         keep = ctx.enter_context(tc.tile_pool(name="keep", bufs=1))
-        stat = ctx.enter_context(tc.tile_pool(name="stat", bufs=4))
+        stat = ctx.enter_context(tc.tile_pool(name="stat", bufs=8))
         psum = ctx.enter_context(tc.psum_pool(name="psum", bufs=8))
 
         ident = keep.tile([P, P], F32, name="ident")
@@ -39,14 +42,14 @@ def tile_layernormgrucell_pa_kernel(tc, x, h, W_irz, b_irz, W_hrz, b_hrz, out_0,
         nc.gpsimd.memset(warm_in[:], 0.0)
         warm_out = keep.tile([P, 1], F32, name="warm_out")
         nc.scalar.activation(out=warm_out[:], in_=warm_in[:], func=AF.Sigmoid)
-        pmax = keep.tile([P, M_TILES], F32, name="pmax")
+        pmax = keep.tile([P, M_TILES + 1], F32, name="pmax")
         o = [keep.tile([P, N], F32, name="o%d" % m) for m in range(M_TILES)]
 
         with ExitStack() as work:
             codes = work.enter_context(tc.tile_pool(name="codes", bufs=1))
-            raw = work.enter_context(tc.tile_pool(name="raw", bufs=8))
+            raw = work.enter_context(tc.tile_pool(name="raw", bufs=6))
             gqp = work.enter_context(tc.tile_pool(name="gqp", bufs=4))
-            zpool = work.enter_context(tc.tile_pool(name="zpool", bufs=3))
+            zpool = work.enter_context(tc.tile_pool(name="zpool", bufs=5))
             junkp = work.enter_context(tc.tile_pool(name="junkp", bufs=2))
 
             wc = [codes.tile([P, 2, N], U32, name="wc%d" % s, align_bytes=64) for s in range(2)]
@@ -55,15 +58,35 @@ def tile_layernormgrucell_pa_kernel(tc, x, h, W_irz, b_irz, W_hrz, b_hrz, out_0,
             xs = [codes.tile([P, 2, ROWS], U8, name="xs%d" % s, align_bytes=64) for s in range(2)]
             bias = [codes.tile([P, N], BF16, name="bias%d" % s) for s in range(2)]
 
-            groups = []
+            brow = codes.tile([P, 2, N], BF16, name="brow")
+            nc.vector.memset(brow[:].rearrange("p s n -> p (s n)").bitcast(I32), 0)
+            ones = codes.tile([P, P], BF16, name="ones")
+            nc.gpsimd.memset(ones[:], 1.0)
+            nc.sync.dma_start(out=brow[0:1, 0, :], in_=b_irz.rearrange("(a n) -> a n", a=1))
+            nc.sync.dma_start(out=brow[0:1, 1, :], in_=b_hrz.rearrange("(a n) -> a n", a=1))
+            pbs = {}
+
+            def bias_matmuls(s):
+                for n in range(N_BANKS):
+                    pb = psum.tile([P, 512], F32, name="pb", tag="bank")
+                    nc.tensor.matmul(out=pb[:], lhsT=ones[:], rhs=brow[:, s, 512 * n:512 * (n + 1)], start=True, stop=True)
+                    pbs[(s, n)] = pb
+
+            def bias_copies(s):
+                for n in range(N_BANKS):
+                    if n % 2 == 0:
+                        nc.scalar.copy(out=bias[s][:, 512 * n:512 * (n + 1)], in_=pbs[(s, n)][:])
+                    else:
+                        nc.vector.tensor_copy(out=bias[s][:, 512 * n:512 * (n + 1)], in_=pbs[(s, n)][:])
+
+            groups = [(x, xc[0], xs[0], 0)]
             for gi in range(4):
                 groups.append((W_irz, wc[0], ws[0], gi))
-            for gi in range(2):
-                groups.append((x, xc[0], xs[0], gi))
+            groups.append((x, xc[0], xs[0], 1))
+            groups.append((h, xc[1], xs[1], 0))
             for gi in range(4):
                 groups.append((W_hrz, wc[1], ws[1], gi))
-            for gi in range(2):
-                groups.append((h, xc[1], xs[1], gi))
+            groups.append((h, xc[1], xs[1], 1))
             n_groups = len(groups)
             rawt = {}
             banks = {}
@@ -105,10 +128,10 @@ def tile_layernormgrucell_pa_kernel(tc, x, h, W_irz, b_irz, W_hrz, b_hrz, out_0,
                 nc.vector.quantize_mx(out=cod[:, g, c0:c0 + 512].bitcast(FP8X4), scales=sca[:, g, c0:c0 + 512], in_=gq[(k, g)][:])
 
             def finish(k):
-                evac(k, 0, 0, False)
-                evac(k, 0, 1, False)
-                evac(k, 1, 0, False)
-                evac(k, 1, 1, True)
+                evac(k, 0, 0, ET_ON_VECTOR[0])
+                evac(k, 0, 1, ET_ON_VECTOR[1])
+                evac(k, 1, 0, ET_ON_VECTOR[2])
+                evac(k, 1, 1, ET_ON_VECTOR[3])
                 quant(k, 0)
                 quant(k, 1)
 
@@ -121,12 +144,13 @@ def tile_layernormgrucell_pa_kernel(tc, x, h, W_irz, b_irz, W_hrz, b_hrz, out_0,
             cc = {}
             qq = {}
 
-            def mx(m, s):
-                tiles = [psum.tile([P, 512], F32, name="acc", tag="bank") for n in range(N_BANKS)]
+            def mx(cells):
+                for cell in cells:
+                    acc[cell] = psum.tile([P, 512], F32, name="acc", tag="bank")
                 for g in range(2):
-                    for n in range(N_BANKS):
+                    for (m, s, n) in cells:
                         nc.tensor.matmul_mx(
-                            out=tiles[n][:],
+                            out=acc[(m, s, n)][:],
                             lhsT=xc[s][:, g, P * m:P * (m + 1)].bitcast(FP8X4),
                             lhsT_scale=xs[s][:, g, P * m:P * (m + 1)],
                             rhs=wc[s][:, g, 512 * n:512 * (n + 1)].bitcast(FP8X4),
@@ -134,29 +158,26 @@ def tile_layernormgrucell_pa_kernel(tc, x, h, W_irz, b_irz, W_hrz, b_hrz, out_0,
                             start=(g == 0),
                             stop=(g == 1),
                         )
-                acc[(m, s)] = tiles
 
-            def evac_z(m, s):
-                if s == 0:
-                    sums[m] = stat.tile([P, 8], F32, name="sums", tag="sums")
-                    negmean[m] = stat.tile([P, 2], F32, name="negmean", tag="negmean")
-                    ssq[m] = stat.tile([P, 2], F32, name="ssq", tag="ssq")
-                    z = o[m]
-                else:
-                    zh[m] = zpool.tile([P, N], F32, name="zh", tag="zh")
-                    z = zh[m]
-                for n in range(N_BANKS):
+            def evac_z(cells):
+                for (m, s, n) in cells:
+                    if m not in sums:
+                        sums[m] = stat.tile([P, 8], F32, name="sums", tag="sums")
+                        negmean[m] = stat.tile([P, 2], F32, name="negmean", tag="negmean")
+                        ssq[m] = stat.tile([P, 2], F32, name="ssq", tag="ssq")
+                    if s == 1 and m not in zh:
+                        zh[m] = zpool.tile([P, N], F32, name="zh", tag="zh")
+                    z = o[m] if s == 0 else zh[m]
                     nc.vector.scalar_tensor_tensor(
-                        out=z[:, 512 * n:512 * (n + 1)], in0=acc[(m, s)][n][:], scalar=1.0,
+                        out=z[:, 512 * n:512 * (n + 1)], in0=acc[(m, s, n)][:], scalar=1.0,
                         in1=bias[s][:, 512 * n:512 * (n + 1)], op0=OP.mult, op1=OP.add,
                         accum_out=sums[m][:, 4 * s + n:4 * s + n + 1])
-                scr = stat.tile([P, 4], F32, name="scr", tag="scr")
-                nc.vector.tensor_scalar(
-                    out=scr[:], in0=sums[m][:, 4 * s:4 * s + 4], scalar1=-1.0 / N, scalar2=None,
-                    op0=OP.mult, op1=OP.add, accum_out=negmean[m][:, s:s + 1])
 
             def square(m, s):
                 z = o[m] if s == 0 else zh[m]
+                scr = stat.tile([P, 4], F32, name="scr", tag="scr")
+                nc.scalar.activation(out=scr[:], in_=sums[m][:, 4 * s:4 * s + 4], func=AF.Copy, scale=-1.0 / N,
+                                     accum_out=negmean[m][:, s:s + 1])
                 junk = junkp.tile([P, N], BF16, name="junk", tag="junk")
                 nc.scalar.activation(out=junk[:], in_=z[:], func=AF.Square, bias=negmean[m][:, s:s + 1], scale=1.0,
                                      accum_out=ssq[m][:, s:s + 1])
@@ -178,53 +199,80 @@ def tile_layernormgrucell_pa_kernel(tc, x, h, W_irz, b_irz, W_hrz, b_hrz, out_0,
                 cc[m] = c
                 qq[m] = q
 
-            def comb(m):
-                nc.vector.scalar_tensor_tensor(out=o[m][:], in0=o[m][:], scalar=qq[m][:, 0:1], in1=zh[m][:],
-                                               op0=OP.mult, op1=OP.add)
+            def finish_tile(m):
+                pieces = 2 if m == M_TILES - 1 else 1
+                wid = N // pieces
+                for c in range(pieces):
+                    ov = o[m][:, wid * c:wid * (c + 1)]
+                    zv = zh[m][:, wid * c:wid * (c + 1)]
+                    if FORMS[m] == "V":
+                        nc.vector.scalar_tensor_tensor(out=ov, in0=ov, scalar=qq[m][:, 0:1], in1=zv, op0=OP.mult, op1=OP.add)
+                    else:
+                        if FORMS[m] == "G":
+                            nc.gpsimd.tensor_scalar(out=ov, in0=ov, scalar1=qq[m][:, 0:1], scalar2=0.0, op0=OP.mult, op1=OP.add)
+                        else:
+                            nc.scalar.activation(out=ov, in_=ov, func=AF.Copy, scale=qq[m][:, 0:1])
+                        nc.gpsimd.tensor_tensor(out=ov, in0=ov, in1=zv, op=OP.add)
+                for c in range(pieces):
+                    ov = o[m][:, wid * c:wid * (c + 1)]
+                    nc.scalar.activation(out=ov, in_=ov, func=AF.Sigmoid, scale=rr[m][:, 1:2], bias=cc[m][:, 0:1])
+                    nc.sync.dma_start(out=out_0[P * m:P * (m + 1), wid * c:wid * (c + 1)], in_=ov)
+                for c in range(pieces):
+                    ov = o[m][:, wid * c:wid * (c + 1)]
+                    nc.vector.tensor_reduce(out=pmax[:, m + c:m + c + 1], in_=ov, op=OP.max, axis=AX.X, apply_absolute_value=True)
 
-            def sig(m):
-                nc.scalar.activation(out=o[m][:], in_=o[m][:], func=AF.Sigmoid, scale=rr[m][:, 1:2], bias=cc[m][:, 0:1])
-                nc.sync.dma_start(out=out_0[P * m:P * (m + 1), :], in_=o[m][:])
+            def by_chunk(s, n):
+                return ("X", [(m, s, n) for m in range(4)])
 
-            def amax(m):
-                nc.vector.tensor_reduce(out=pmax[:, m:m + 1], in_=o[m][:], op=OP.max, axis=AX.X, apply_absolute_value=True)
+            def by_tile(s, m):
+                return ("X", [(m, s, n) for n in range(N_BANKS)])
 
-            for k in range(4):
+            jobs = [("T", 0), ("B", 0), ("T", 1), ("B", 1), ("T", 2)]
+            for n in range(4):
+                jobs.append(by_chunk(0, n))
+                jobs.append(("T", 3 + n))
+            for m in range(4, 8):
+                jobs.append(by_tile(0, m))
+                jobs.append(("T", 3 + m))
+            jobs.append(by_chunk(1, 0))
+            jobs.append(("T", 11))
+            for n in range(1, 4):
+                jobs.append(by_chunk(1, n))
+            for m in range(4, 8):
+                jobs.append(by_tile(1, m))
+
+            def issue(job):
+                if job[0] == "T":
+                    transposes(job[1])
+                elif job[0] == "B":
+                    bias_matmuls(job[1])
+                else:
+                    mx(job[1])
+
+            seen = {}
+            for k in range(3):
                 load(k)
-            transposes(0)
-            transposes(1)
-            for k in range(n_groups):
-                finish(k)
-                if k + 4 < n_groups:
-                    load(k + 4)
-                if k + 4 == n_groups:
-                    nc.sync.dma_start(out=bias[0][:], in_=b_irz.partition_broadcast(P))
-                    nc.sync.dma_start(out=bias[1][:], in_=b_hrz.partition_broadcast(P))
-                if k + 2 < n_groups:
-                    transposes(k + 2)
-                if k + 2 == n_groups:
-                    mx(0, 0)
-            mx(0, 1)
-
-            for m in range(M_TILES):
-                evac_z(m, 0)
-                square(m, 0)
-                if m + 1 < M_TILES:
-                    mx(m + 1, 0)
-                if m >= 2:
-                    amax(m - 2)
-                evac_z(m, 1)
-                square(m, 1)
-                if m + 1 < M_TILES:
-                    mx(m + 1, 1)
-                chain(m)
-                if m >= 1:
-                    comb(m - 1)
-                    sig(m - 1)
-            amax(M_TILES - 2)
-            comb(M_TILES - 1)
-            sig(M_TILES - 1)
-            amax(M_TILES - 1)
+            issue(jobs[0])
+            issue(jobs[1])
+            for i in range(len(jobs)):
+                kind = jobs[i][0]
+                if kind == "T":
+                    finish(jobs[i][1])
+                    if jobs[i][1] + 3 < n_groups:
+                        load(jobs[i][1] + 3)
+                elif kind == "B":
+                    bias_copies(jobs[i][1])
+                else:
+                    evac_z(jobs[i][1])
+                    for (m, s, n) in jobs[i][1]:
+                        seen[(m, s)] = seen.get((m, s), 0) + 1
+                        if seen[(m, s)] == N_BANKS:
+                            square(m, s)
+                            if s == 1:
+                                chain(m)
+                                finish_tile(m)
+                if i + 2 < len(jobs):
+                    issue(jobs[i + 2])
 
         part = stat.tile([P, 1], F32, name="part", tag="part")
         nc.vector.tensor_reduce(out=part[:], in_=pmax[:], op=OP.max, axis=AX.X)

@@ -7,7 +7,6 @@ F32 = mybir.dt.float32
 BF16 = mybir.dt.bfloat16
 U32 = mybir.dt.uint32
 U8 = mybir.dt.uint8
-I32 = mybir.dt.int32
 FP8X4 = mybir.dt.float8_e4m3fn_x4
 FP8 = mybir.dt.float8_e4m3fn
 AF = mybir.ActivationFunctionType
@@ -23,13 +22,17 @@ FLOPS = 2 * 2 * ROWS * K * N
 M_TILES = ROWS // P
 N_BANKS = N // 512
 CV = 1344
-FORMS = ("V", "V", "V", "V", "V", "V", "V", "V")
-ET_ON_VECTOR = (False, False, False, True)
+FORMS = ("G", "G", "V", "G", "G", "V", "G", "V")
+LAGS = {"V": (4, 0, 3), "G": (0, 5, 3)}
+ET_ON_VECTOR = (True, False, False, False)
+BIAS_AFTER = (1, 5)
+LOAD_AHEAD = 3
 
 
 def tile_layernormgrucell_pa_kernel(tc, x, h, W_irz, b_irz, W_hrz, b_hrz, out_0, out_1):
     nc = tc.nc
     with ExitStack() as ctx:
+        ctx.enter_context(tc.manual_schedule())
         keep = ctx.enter_context(tc.tile_pool(name="keep", bufs=1))
         stat = ctx.enter_context(tc.tile_pool(name="stat", bufs=8))
         psum = ctx.enter_context(tc.psum_pool(name="psum", bufs=8))
@@ -47,23 +50,21 @@ def tile_layernormgrucell_pa_kernel(tc, x, h, W_irz, b_irz, W_hrz, b_hrz, out_0,
 
         with ExitStack() as work:
             codes = work.enter_context(tc.tile_pool(name="codes", bufs=1))
-            raw = work.enter_context(tc.tile_pool(name="raw", bufs=6))
-            gqp = work.enter_context(tc.tile_pool(name="gqp", bufs=4))
+            raw = work.enter_context(tc.tile_pool(name="raw", bufs=2 * LOAD_AHEAD))
+            gqp = work.enter_context(tc.tile_pool(name="gqp", bufs=2))
             zpool = work.enter_context(tc.tile_pool(name="zpool", bufs=5))
             junkp = work.enter_context(tc.tile_pool(name="junkp", bufs=2))
 
-            wc = [codes.tile([P, 2, N], U32, name="wc%d" % s, align_bytes=64) for s in range(2)]
-            ws = [codes.tile([P, 2, N], U8, name="ws%d" % s, align_bytes=64) for s in range(2)]
-            xc = [codes.tile([P, 2, ROWS], U32, name="xc%d" % s, align_bytes=64) for s in range(2)]
-            xs = [codes.tile([P, 2, ROWS], U8, name="xs%d" % s, align_bytes=64) for s in range(2)]
+            wc = [codes.tile([P, N // 512, 2, 512], U32, name="wc%d" % s, align_bytes=64) for s in range(2)]
+            ws = [codes.tile([P, N // 512, 2, 512], U8, name="ws%d" % s, align_bytes=64) for s in range(2)]
+            xc = [codes.tile([P, ROWS // 512, 2, 512], U32, name="xc%d" % s, align_bytes=64) for s in range(2)]
+            xs = [codes.tile([P, ROWS // 512, 2, 512], U8, name="xs%d" % s, align_bytes=64) for s in range(2)]
             bias = [codes.tile([P, N], BF16, name="bias%d" % s) for s in range(2)]
 
             brow = codes.tile([P, 2, N], BF16, name="brow")
-            nc.vector.memset(brow[:].rearrange("p s n -> p (s n)").bitcast(I32), 0)
+            nc.gpsimd.memset(brow[:], 0.0)
             ones = codes.tile([P, P], BF16, name="ones")
             nc.gpsimd.memset(ones[:], 1.0)
-            nc.sync.dma_start(out=brow[0:1, 0, :], in_=b_irz.rearrange("(a n) -> a n", a=1))
-            nc.sync.dma_start(out=brow[0:1, 1, :], in_=b_hrz.rearrange("(a n) -> a n", a=1))
             pbs = {}
 
             def bias_matmuls(s):
@@ -74,19 +75,17 @@ def tile_layernormgrucell_pa_kernel(tc, x, h, W_irz, b_irz, W_hrz, b_hrz, out_0,
 
             def bias_copies(s):
                 for n in range(N_BANKS):
-                    if n % 2 == 0:
-                        nc.scalar.copy(out=bias[s][:, 512 * n:512 * (n + 1)], in_=pbs[(s, n)][:])
-                    else:
-                        nc.vector.tensor_copy(out=bias[s][:, 512 * n:512 * (n + 1)], in_=pbs[(s, n)][:])
+                    nc.scalar.copy(out=bias[s][:, 512 * n:512 * (n + 1)], in_=pbs[(s, n)][:])
 
-            groups = [(x, xc[0], xs[0], 0)]
+            groups = []
             for gi in range(4):
                 groups.append((W_irz, wc[0], ws[0], gi))
-            groups.append((x, xc[0], xs[0], 1))
-            groups.append((h, xc[1], xs[1], 0))
+            for gi in range(2):
+                groups.append((x, xc[0], xs[0], gi))
             for gi in range(4):
                 groups.append((W_hrz, wc[1], ws[1], gi))
-            groups.append((h, xc[1], xs[1], 1))
+            for gi in range(2):
+                groups.append((h, xc[1], xs[1], gi))
             n_groups = len(groups)
             rawt = {}
             banks = {}
@@ -98,7 +97,7 @@ def tile_layernormgrucell_pa_kernel(tc, x, h, W_irz, b_irz, W_hrz, b_hrz, out_0,
                 for j in range(2):
                     r = raw.tile([P, 2, K], BF16, name="raw", tag="raw")
                     r0 = (4 * gi + 2 * j) * P
-                    nc.sync.dma_start(out=r[:], in_=src[r0:r0 + 2 * P, :].rearrange("(t p) k -> p t k", p=P))
+                    nc.sync.dma_start(out=r[:], in_=src[r0:r0 + 2 * P, :].rearrange("(p t) k -> p t k", p=P))
                     rawt[(k, j)] = r
 
             def transposes(k):
@@ -112,28 +111,25 @@ def tile_layernormgrucell_pa_kernel(tc, x, h, W_irz, b_irz, W_hrz, b_hrz, out_0,
                         banks[(k, j, g)] = bank
 
             def evac(k, j, g, on_vector):
-                if (k, g) not in gq:
-                    gq[(k, g)] = gqp.tile([P, 2048], BF16, name="gq", tag="gq", align_bytes=64)
-                dst = gq[(k, g)][:, 1024 * j:1024 * (j + 1)].bitcast(F32).rearrange("p (t r u) -> p t r u", t=2, u=2)
-                src = banks[(k, j, g)][:].rearrange("p t u r -> p t r u")
+                dst = gq[k][:, g, 1024 * j:1024 * (j + 1)].bitcast(F32).rearrange("p (r t u) -> p r t u", t=2, u=2)
+                src = banks[(k, j, g)][:].rearrange("p t u r -> p r t u")
                 if on_vector:
                     nc.vector.tensor_copy(out=dst, in_=src)
                 else:
                     nc.scalar.copy(out=dst, in_=src)
 
-            def quant(k, g):
-                cod = groups[k][1]
-                sca = groups[k][2]
-                c0 = 512 * groups[k][3]
-                nc.vector.quantize_mx(out=cod[:, g, c0:c0 + 512].bitcast(FP8X4), scales=sca[:, g, c0:c0 + 512], in_=gq[(k, g)][:])
-
             def finish(k):
+                gq[k] = gqp.tile([P, 2, 2048], BF16, name="gq", tag="gq", align_bytes=64)
                 evac(k, 0, 0, ET_ON_VECTOR[0])
                 evac(k, 0, 1, ET_ON_VECTOR[1])
                 evac(k, 1, 0, ET_ON_VECTOR[2])
                 evac(k, 1, 1, ET_ON_VECTOR[3])
-                quant(k, 0)
-                quant(k, 1)
+                cod = groups[k][1]
+                sca = groups[k][2]
+                gi = groups[k][3]
+                nc.vector.quantize_mx(out=cod[:, gi, :, :].rearrange("p g c -> p (g c)").bitcast(FP8X4),
+                                      scales=sca[:, gi, :, :].rearrange("p g c -> p (g c)"),
+                                      in_=gq[k][:].rearrange("p g c -> p (g c)"))
 
             acc = {}
             zh = {}
@@ -144,32 +140,33 @@ def tile_layernormgrucell_pa_kernel(tc, x, h, W_irz, b_irz, W_hrz, b_hrz, out_0,
             cc = {}
             qq = {}
 
-            def mx(cells):
-                for cell in cells:
-                    acc[cell] = psum.tile([P, 512], F32, name="acc", tag="bank")
+            def mx(m, s):
+                tiles = [psum.tile([P, 512], F32, name="acc", tag="bank") for n in range(N_BANKS)]
                 for g in range(2):
-                    for (m, s, n) in cells:
+                    for n in range(N_BANKS):
                         nc.tensor.matmul_mx(
-                            out=acc[(m, s, n)][:],
-                            lhsT=xc[s][:, g, P * m:P * (m + 1)].bitcast(FP8X4),
-                            lhsT_scale=xs[s][:, g, P * m:P * (m + 1)],
-                            rhs=wc[s][:, g, 512 * n:512 * (n + 1)].bitcast(FP8X4),
-                            rhs_scale=ws[s][:, g, 512 * n:512 * (n + 1)],
+                            out=tiles[n][:],
+                            lhsT=xc[s][:, m // 4, g, P * (m % 4):P * (m % 4 + 1)].bitcast(FP8X4),
+                            lhsT_scale=xs[s][:, m // 4, g, P * (m % 4):P * (m % 4 + 1)],
+                            rhs=wc[s][:, n, g, :].bitcast(FP8X4),
+                            rhs_scale=ws[s][:, n, g, :],
                             start=(g == 0),
                             stop=(g == 1),
                         )
+                acc[(m, s)] = tiles
 
-            def evac_z(cells):
-                for (m, s, n) in cells:
-                    if m not in sums:
-                        sums[m] = stat.tile([P, 8], F32, name="sums", tag="sums")
-                        negmean[m] = stat.tile([P, 2], F32, name="negmean", tag="negmean")
-                        ssq[m] = stat.tile([P, 2], F32, name="ssq", tag="ssq")
-                    if s == 1 and m not in zh:
-                        zh[m] = zpool.tile([P, N], F32, name="zh", tag="zh")
-                    z = o[m] if s == 0 else zh[m]
+            def evac_z(m, s):
+                if s == 0:
+                    sums[m] = stat.tile([P, 8], F32, name="sums", tag="sums")
+                    negmean[m] = stat.tile([P, 2], F32, name="negmean", tag="negmean")
+                    ssq[m] = stat.tile([P, 2], F32, name="ssq", tag="ssq")
+                    z = o[m]
+                else:
+                    zh[m] = zpool.tile([P, N], F32, name="zh", tag="zh")
+                    z = zh[m]
+                for n in range(N_BANKS):
                     nc.vector.scalar_tensor_tensor(
-                        out=z[:, 512 * n:512 * (n + 1)], in0=acc[(m, s, n)][:], scalar=1.0,
+                        out=z[:, 512 * n:512 * (n + 1)], in0=acc[(m, s)][n][:], scalar=1.0,
                         in1=bias[s][:, 512 * n:512 * (n + 1)], op0=OP.mult, op1=OP.add,
                         accum_out=sums[m][:, 4 * s + n:4 * s + n + 1])
 
@@ -199,47 +196,42 @@ def tile_layernormgrucell_pa_kernel(tc, x, h, W_irz, b_irz, W_hrz, b_hrz, out_0,
                 cc[m] = c
                 qq[m] = q
 
-            def finish_tile(m):
-                pieces = 2 if m == M_TILES - 1 else 1
-                wid = N // pieces
-                for c in range(pieces):
-                    ov = o[m][:, wid * c:wid * (c + 1)]
-                    zv = zh[m][:, wid * c:wid * (c + 1)]
+            def pieces_of(m):
+                n_pieces = 2 if m == M_TILES - 1 else 1
+                wid = N // n_pieces
+                return [slice(wid * c, wid * (c + 1)) for c in range(n_pieces)]
+
+            def comb(m):
+                for cols in pieces_of(m):
                     if FORMS[m] == "V":
-                        nc.vector.scalar_tensor_tensor(out=ov, in0=ov, scalar=qq[m][:, 0:1], in1=zv, op0=OP.mult, op1=OP.add)
+                        nc.vector.scalar_tensor_tensor(out=o[m][:, cols], in0=o[m][:, cols], scalar=qq[m][:, 0:1],
+                                                       in1=zh[m][:, cols], op0=OP.mult, op1=OP.add)
                     else:
-                        if FORMS[m] == "G":
-                            nc.gpsimd.tensor_scalar(out=ov, in0=ov, scalar1=qq[m][:, 0:1], scalar2=0.0, op0=OP.mult, op1=OP.add)
-                        else:
-                            nc.scalar.activation(out=ov, in_=ov, func=AF.Copy, scale=qq[m][:, 0:1])
-                        nc.gpsimd.tensor_tensor(out=ov, in0=ov, in1=zv, op=OP.add)
-                for c in range(pieces):
-                    ov = o[m][:, wid * c:wid * (c + 1)]
-                    nc.scalar.activation(out=ov, in_=ov, func=AF.Sigmoid, scale=rr[m][:, 1:2], bias=cc[m][:, 0:1])
-                    nc.sync.dma_start(out=out_0[P * m:P * (m + 1), wid * c:wid * (c + 1)], in_=ov)
-                for c in range(pieces):
-                    ov = o[m][:, wid * c:wid * (c + 1)]
-                    nc.vector.tensor_reduce(out=pmax[:, m + c:m + c + 1], in_=ov, op=OP.max, axis=AX.X, apply_absolute_value=True)
+                        nc.gpsimd.tensor_scalar(out=o[m][:, cols], in0=o[m][:, cols], scalar1=qq[m][:, 0:1], scalar2=0.0,
+                                                op0=OP.mult, op1=OP.add)
+                        nc.gpsimd.tensor_tensor(out=o[m][:, cols], in0=o[m][:, cols], in1=zh[m][:, cols], op=OP.add)
 
-            def by_chunk(s, n):
-                return ("X", [(m, s, n) for m in range(4)])
+            def sig(m):
+                for cols in pieces_of(m):
+                    nc.scalar.activation(out=o[m][:, cols], in_=o[m][:, cols], func=AF.Sigmoid, scale=rr[m][:, 1:2],
+                                         bias=cc[m][:, 0:1])
+                    nc.sync.dma_start(out=out_0[P * m:P * (m + 1), cols], in_=o[m][:, cols])
 
-            def by_tile(s, m):
-                return ("X", [(m, s, n) for n in range(N_BANKS)])
+            def amax(m):
+                c = 0
+                for cols in pieces_of(m):
+                    nc.vector.tensor_reduce(out=pmax[:, m + c:m + c + 1], in_=o[m][:, cols], op=OP.max, axis=AX.X,
+                                            apply_absolute_value=True)
+                    c += 1
 
-            jobs = [("T", 0), ("B", 0), ("T", 1), ("B", 1), ("T", 2)]
-            for n in range(4):
-                jobs.append(by_chunk(0, n))
-                jobs.append(("T", 3 + n))
-            for m in range(4, 8):
-                jobs.append(by_tile(0, m))
-                jobs.append(("T", 3 + m))
-            jobs.append(by_chunk(1, 0))
-            jobs.append(("T", 11))
-            for n in range(1, 4):
-                jobs.append(by_chunk(1, n))
-            for m in range(4, 8):
-                jobs.append(by_tile(1, m))
+            jobs = []
+            for k in range(n_groups):
+                jobs.append(("T", k))
+                if k in BIAS_AFTER:
+                    jobs.append(("B", BIAS_AFTER.index(k)))
+            for m in range(M_TILES):
+                jobs.append(("I", m))
+                jobs.append(("H", m))
 
             def issue(job):
                 if job[0] == "T":
@@ -247,32 +239,51 @@ def tile_layernormgrucell_pa_kernel(tc, x, h, W_irz, b_irz, W_hrz, b_hrz, out_0,
                 elif job[0] == "B":
                     bias_matmuls(job[1])
                 else:
-                    mx(job[1])
+                    mx(job[1], 0 if job[0] == "I" else 1)
 
-            seen = {}
-            for k in range(3):
+            events = []
+
+            def run_events(limit):
+                due = sorted([e for e in events if limit is None or e[0] <= limit])
+                for e in due:
+                    events.remove(e)
+                    if e[1] == 0:
+                        amax(e[2])
+                    elif e[1] == 1:
+                        comb(e[2])
+                    else:
+                        sig(e[2])
+
+            for k in range(LOAD_AHEAD):
                 load(k)
+            nc.sync.dma_start(out=brow[0:1, 0, :], in_=b_irz.rearrange("(a n) -> a n", a=1))
+            nc.sync.dma_start(out=brow[0:1, 1, :], in_=b_hrz.rearrange("(a n) -> a n", a=1))
             issue(jobs[0])
             issue(jobs[1])
             for i in range(len(jobs)):
                 kind = jobs[i][0]
+                idx = jobs[i][1]
                 if kind == "T":
-                    finish(jobs[i][1])
-                    if jobs[i][1] + 3 < n_groups:
-                        load(jobs[i][1] + 3)
+                    finish(idx)
+                    if idx + LOAD_AHEAD < n_groups:
+                        load(idx + LOAD_AHEAD)
                 elif kind == "B":
-                    bias_copies(jobs[i][1])
+                    bias_copies(idx)
+                elif kind == "I":
+                    evac_z(idx, 0)
+                    square(idx, 0)
                 else:
-                    evac_z(jobs[i][1])
-                    for (m, s, n) in jobs[i][1]:
-                        seen[(m, s)] = seen.get((m, s), 0) + 1
-                        if seen[(m, s)] == N_BANKS:
-                            square(m, s)
-                            if s == 1:
-                                chain(m)
-                                finish_tile(m)
+                    evac_z(idx, 1)
+                    square(idx, 1)
+                    chain(idx)
+                    lag = LAGS[FORMS[idx]]
+                    events.append((i + lag[0], 1, idx))
+                    events.append((i + lag[0] + lag[1], 2, idx))
+                    events.append((i + lag[0] + lag[1] + lag[2], 0, idx))
                 if i + 2 < len(jobs):
                     issue(jobs[i + 2])
+                run_events(i)
+            run_events(None)
 
         part = stat.tile([P, 1], F32, name="part", tag="part")
         nc.vector.tensor_reduce(out=part[:], in_=pmax[:], op=OP.max, axis=AX.X)

from contextlib import ExitStack

import concourse.mybir as mybir
from concourse.masks import make_identity

F32 = mybir.dt.float32
BF16 = mybir.dt.bfloat16
U32 = mybir.dt.uint32
U8 = mybir.dt.uint8
FP8X4 = mybir.dt.float8_e4m3fn_x4
FP8 = mybir.dt.float8_e4m3fn
AF = mybir.ActivationFunctionType
OP = mybir.AluOpType
AX = mybir.AxisListType

P = 128
ROWS = 1024
K = 1024
N = 2048
EPS = 1e-5
FLOPS = 2 * 2 * ROWS * K * N
M_TILES = ROWS // P
N_BANKS = N // 512
CV = 1344
FORMS = ("G", "G", "V", "G", "G", "V", "G", "V")
LAGS = {"V": (4, 0, 3), "G": (0, 5, 3)}
ET_ON_VECTOR = (True, False, False, False)
BIAS_AFTER = (1, 5)
LOAD_AHEAD = 3


def tile_layernormgrucell_pa_kernel(tc, x, h, W_irz, b_irz, W_hrz, b_hrz, out_0, out_1):
    nc = tc.nc
    with ExitStack() as ctx:
        ctx.enter_context(tc.manual_schedule())
        keep = ctx.enter_context(tc.tile_pool(name="keep", bufs=1))
        stat = ctx.enter_context(tc.tile_pool(name="stat", bufs=8))
        psum = ctx.enter_context(tc.psum_pool(name="psum", bufs=8))

        ident = keep.tile([P, P], F32, name="ident")
        make_identity(nc, ident[:])
        mhalf = keep.tile([P, 2], F32, name="mhalf")
        nc.gpsimd.memset(mhalf[:], -0.5)
        warm_in = keep.tile([P, 1], F32, name="warm_in")
        nc.gpsimd.memset(warm_in[:], 0.0)
        warm_out = keep.tile([P, 1], F32, name="warm_out")
        nc.scalar.activation(out=warm_out[:], in_=warm_in[:], func=AF.Sigmoid)
        pmax = keep.tile([P, M_TILES + 1], F32, name="pmax")
        o = [keep.tile([P, N], F32, name="o%d" % m) for m in range(M_TILES)]

        with ExitStack() as work:
            codes = work.enter_context(tc.tile_pool(name="codes", bufs=1))
            raw = work.enter_context(tc.tile_pool(name="raw", bufs=2 * LOAD_AHEAD))
            gqp = work.enter_context(tc.tile_pool(name="gqp", bufs=2))
            zpool = work.enter_context(tc.tile_pool(name="zpool", bufs=5))
            junkp = work.enter_context(tc.tile_pool(name="junkp", bufs=2))

            wc = [codes.tile([P, N // 512, 2, 512], U32, name="wc%d" % s, align_bytes=64) for s in range(2)]
            ws = [codes.tile([P, N // 512, 2, 512], U8, name="ws%d" % s, align_bytes=64) for s in range(2)]
            xc = [codes.tile([P, ROWS // 512, 2, 512], U32, name="xc%d" % s, align_bytes=64) for s in range(2)]
            xs = [codes.tile([P, ROWS // 512, 2, 512], U8, name="xs%d" % s, align_bytes=64) for s in range(2)]
            bias = [codes.tile([P, N], BF16, name="bias%d" % s) for s in range(2)]

            brow = codes.tile([P, 2, N], BF16, name="brow")
            nc.gpsimd.memset(brow[:], 0.0)
            ones = codes.tile([P, P], BF16, name="ones")
            nc.gpsimd.memset(ones[:], 1.0)
            pbs = {}

            def bias_matmuls(s):
                for n in range(N_BANKS):
                    pb = psum.tile([P, 512], F32, name="pb", tag="bank")
                    nc.tensor.matmul(out=pb[:], lhsT=ones[:], rhs=brow[:, s, 512 * n:512 * (n + 1)], start=True, stop=True)
                    pbs[(s, n)] = pb

            def bias_copies(s):
                for n in range(N_BANKS):
                    nc.scalar.copy(out=bias[s][:, 512 * n:512 * (n + 1)], in_=pbs[(s, n)][:])

            groups = []
            for gi in range(4):
                groups.append((W_irz, wc[0], ws[0], gi))
            for gi in range(2):
                groups.append((x, xc[0], xs[0], gi))
            for gi in range(4):
                groups.append((W_hrz, wc[1], ws[1], gi))
            for gi in range(2):
                groups.append((h, xc[1], xs[1], gi))
            n_groups = len(groups)
            rawt = {}
            banks = {}
            gq = {}

            def load(k):
                src = groups[k][0]
                gi = groups[k][3]
                for j in range(2):
                    r = raw.tile([P, 2, K], BF16, name="raw", tag="raw")
                    r0 = (4 * gi + 2 * j) * P
                    nc.sync.dma_start(out=r[:], in_=src[r0:r0 + 2 * P, :].rearrange("(p t) k -> p t k", p=P))
                    rawt[(k, j)] = r

            def transposes(k):
                for j in range(2):
                    words = rawt[(k, j)][:].bitcast(F32)
                    for g in range(2):
                        bank = psum.tile([P, 2, 2, P], F32, name="bank", tag="bank")
                        for t in range(2):
                            for u in range(2):
                                nc.tensor.transpose(bank[:, t, u, :], words[:, t, 256 * g + u:256 * (g + 1):2], ident[:])
                        banks[(k, j, g)] = bank

            def evac(k, j, g, on_vector):
                dst = gq[k][:, g, 1024 * j:1024 * (j + 1)].bitcast(F32).rearrange("p (r t u) -> p r t u", t=2, u=2)
                src = banks[(k, j, g)][:].rearrange("p t u r -> p r t u")
                if on_vector:
                    nc.vector.tensor_copy(out=dst, in_=src)
                else:
                    nc.scalar.copy(out=dst, in_=src)

            def finish(k):
                gq[k] = gqp.tile([P, 2, 2048], BF16, name="gq", tag="gq", align_bytes=64)
                evac(k, 0, 0, ET_ON_VECTOR[0])
                evac(k, 0, 1, ET_ON_VECTOR[1])
                evac(k, 1, 0, ET_ON_VECTOR[2])
                evac(k, 1, 1, ET_ON_VECTOR[3])
                cod = groups[k][1]
                sca = groups[k][2]
                gi = groups[k][3]
                nc.vector.quantize_mx(out=cod[:, gi, :, :].rearrange("p g c -> p (g c)").bitcast(FP8X4),
                                      scales=sca[:, gi, :, :].rearrange("p g c -> p (g c)"),
                                      in_=gq[k][:].rearrange("p g c -> p (g c)"))

            acc = {}
            zh = {}
            sums = {}
            negmean = {}
            ssq = {}
            rr = {}
            cc = {}
            qq = {}

            def mx(m, s):
                tiles = [psum.tile([P, 512], F32, name="acc", tag="bank") for n in range(N_BANKS)]
                for g in range(2):
                    for n in range(N_BANKS):
                        nc.tensor.matmul_mx(
                            out=tiles[n][:],
                            lhsT=xc[s][:, m // 4, g, P * (m % 4):P * (m % 4 + 1)].bitcast(FP8X4),
                            lhsT_scale=xs[s][:, m // 4, g, P * (m % 4):P * (m % 4 + 1)],
                            rhs=wc[s][:, n, g, :].bitcast(FP8X4),
                            rhs_scale=ws[s][:, n, g, :],
                            start=(g == 0),
                            stop=(g == 1),
                        )
                acc[(m, s)] = tiles

            def evac_z(m, s):
                if s == 0:
                    sums[m] = stat.tile([P, 8], F32, name="sums", tag="sums")
                    negmean[m] = stat.tile([P, 2], F32, name="negmean", tag="negmean")
                    ssq[m] = stat.tile([P, 2], F32, name="ssq", tag="ssq")
                    z = o[m]
                else:
                    zh[m] = zpool.tile([P, N], F32, name="zh", tag="zh")
                    z = zh[m]
                for n in range(N_BANKS):
                    nc.vector.scalar_tensor_tensor(
                        out=z[:, 512 * n:512 * (n + 1)], in0=acc[(m, s)][n][:], scalar=1.0,
                        in1=bias[s][:, 512 * n:512 * (n + 1)], op0=OP.mult, op1=OP.add,
                        accum_out=sums[m][:, 4 * s + n:4 * s + n + 1])

            def square(m, s):
                z = o[m] if s == 0 else zh[m]
                scr = stat.tile([P, 4], F32, name="scr", tag="scr")
                nc.scalar.activation(out=scr[:], in_=sums[m][:, 4 * s:4 * s + 4], func=AF.Copy, scale=-1.0 / N,
                                     accum_out=negmean[m][:, s:s + 1])
                junk = junkp.tile([P, N], BF16, name="junk", tag="junk")
                nc.scalar.activation(out=junk[:], in_=z[:], func=AF.Square, bias=negmean[m][:, s:s + 1], scale=1.0,
                                     accum_out=ssq[m][:, s:s + 1])

            def chain(m):
                ve = stat.tile([P, 2], F32, name="ve", tag="ve")
                nc.gpsimd.tensor_scalar(out=ve[:], in0=ssq[m][:], scalar1=1.0 / N, scalar2=EPS, op0=OP.mult, op1=OP.add)
                r = stat.tile([P, 2], F32, name="r", tag="r")
                nc.gpsimd.tensor_tensor(out=r[:], in0=ve[:], in1=mhalf[:], op=OP.pow)
                pr = stat.tile([P, 2], F32, name="pr", tag="pr")
                nc.gpsimd.tensor_tensor(out=pr[:], in0=negmean[m][:], in1=r[:], op=OP.mult)
                c = stat.tile([P, 1], F32, name="c", tag="c")
                nc.gpsimd.tensor_tensor(out=c[:], in0=pr[:, 0:1], in1=pr[:, 1:2], op=OP.add)
                a = stat.tile([P, 1], F32, name="a", tag="a")
                nc.gpsimd.tensor_tensor(out=a[:], in0=r[:, 0:1], in1=r[:, 1:2], op=OP.mult)
                q = stat.tile([P, 1], F32, name="q", tag="q")
                nc.gpsimd.tensor_tensor(out=q[:], in0=a[:], in1=ve[:, 1:2], op=OP.mult)
                rr[m] = r
                cc[m] = c
                qq[m] = q

            def pieces_of(m):
                n_pieces = 2 if m == M_TILES - 1 else 1
                wid = N // n_pieces
                return [slice(wid * c, wid * (c + 1)) for c in range(n_pieces)]

            def comb(m):
                for cols in pieces_of(m):
                    if FORMS[m] == "V":
                        nc.vector.scalar_tensor_tensor(out=o[m][:, cols], in0=o[m][:, cols], scalar=qq[m][:, 0:1],
                                                       in1=zh[m][:, cols], op0=OP.mult, op1=OP.add)
                    else:
                        nc.gpsimd.tensor_scalar(out=o[m][:, cols], in0=o[m][:, cols], scalar1=qq[m][:, 0:1], scalar2=0.0,
                                                op0=OP.mult, op1=OP.add)
                        nc.gpsimd.tensor_tensor(out=o[m][:, cols], in0=o[m][:, cols], in1=zh[m][:, cols], op=OP.add)

            def sig(m):
                for cols in pieces_of(m):
                    nc.scalar.activation(out=o[m][:, cols], in_=o[m][:, cols], func=AF.Sigmoid, scale=rr[m][:, 1:2],
                                         bias=cc[m][:, 0:1])
                    nc.sync.dma_start(out=out_0[P * m:P * (m + 1), cols], in_=o[m][:, cols])

            def amax(m):
                c = 0
                for cols in pieces_of(m):
                    nc.vector.tensor_reduce(out=pmax[:, m + c:m + c + 1], in_=o[m][:, cols], op=OP.max, axis=AX.X,
                                            apply_absolute_value=True)
                    c += 1

            jobs = []
            for k in range(n_groups):
                jobs.append(("T", k))
                if k in BIAS_AFTER:
                    jobs.append(("B", BIAS_AFTER.index(k)))
            for m in range(M_TILES):
                jobs.append(("I", m))
                jobs.append(("H", m))

            def issue(job):
                if job[0] == "T":
                    transposes(job[1])
                elif job[0] == "B":
                    bias_matmuls(job[1])
                else:
                    mx(job[1], 0 if job[0] == "I" else 1)

            events = []

            def run_events(limit):
                due = sorted([e for e in events if limit is None or e[0] <= limit])
                for e in due:
                    events.remove(e)
                    if e[1] == 0:
                        amax(e[2])
                    elif e[1] == 1:
                        comb(e[2])
                    else:
                        sig(e[2])

            for k in range(LOAD_AHEAD):
                load(k)
            nc.sync.dma_start(out=brow[0:1, 0, :], in_=b_irz.rearrange("(a n) -> a n", a=1))
            nc.sync.dma_start(out=brow[0:1, 1, :], in_=b_hrz.rearrange("(a n) -> a n", a=1))
            issue(jobs[0])
            issue(jobs[1])
            for i in range(len(jobs)):
                kind = jobs[i][0]
                idx = jobs[i][1]
                if kind == "T":
                    finish(idx)
                    if idx + LOAD_AHEAD < n_groups:
                        load(idx + LOAD_AHEAD)
                elif kind == "B":
                    bias_copies(idx)
                elif kind == "I":
                    evac_z(idx, 0)
                    square(idx, 0)
                else:
                    evac_z(idx, 1)
                    square(idx, 1)
                    chain(idx)
                    lag = LAGS[FORMS[idx]]
                    events.append((i + lag[0], 1, idx))
                    events.append((i + lag[0] + lag[1], 2, idx))
                    events.append((i + lag[0] + lag[1] + lag[2], 0, idx))
                if i + 2 < len(jobs):
                    issue(jobs[i + 2])
                run_events(i)
            run_events(None)

        part = stat.tile([P, 1], F32, name="part", tag="part")
        nc.vector.tensor_reduce(out=part[:], in_=pmax[:], op=OP.max, axis=AX.X)
        spread = psum.tile([P, 512], F32, name="spread", tag="bank")
        nc.tensor.transpose(spread[:, 0:P], part[:, 0:1].to_broadcast([P, P]), ident[:])
        top = stat.tile([P, 1], F32, name="top", tag="top")
        nc.vector.tensor_reduce(out=top[:], in_=spread[:, 0:P], op=OP.max, axis=AX.X)
        rec = stat.tile([P, 1], F32, name="rec", tag="rec")
        nc.vector.reciprocal(out=rec[:], in_=top[:])
        fac = stat.tile([P, 1], F32, name="fac", tag="fac")
        nc.vector.tensor_scalar(out=fac[:], in0=rec[:], scalar1=448.0, scalar2=None, op0=OP.mult)

        scp = ctx.enter_context(tc.tile_pool(name="scp", bufs=3))
        o8p = ctx.enter_context(tc.tile_pool(name="o8p", bufs=4))
        sc = {}
        o8 = {}

        def scale2(m):
            sc[m] = scp.tile([P, N], F32, name="sc", tag="sc")
            nc.vector.tensor_scalar(out=sc[m][:, 0:CV], in0=o[m][:, 0:CV], scalar1=fac[:, 0:1], scalar2=None, op0=OP.mult)
            nc.scalar.activation(out=sc[m][:, CV:N], in_=o[m][:, CV:N], func=AF.Copy, scale=fac[:, 0:1])

        def cast2(m):
            o8[m] = o8p.tile([P, N], FP8, name="o8", tag="o8")
            nc.vector.tensor_copy(out=o8[m][:, 0:CV], in_=sc[m][:, 0:CV], saturate=False)
            nc.scalar.copy(out=o8[m][:, CV:N], in_=sc[m][:, CV:N], saturate=False)
            nc.sync.dma_start(out=out_1[P * m:P * (m + 1), :], in_=o8[m][:].bitcast(U8))

        scale2(0)
        for m in range(M_TILES):
            if m + 1 < M_TILES:
                scale2(m + 1)
            cast2(m)
